import numpy as np
import ml_dtypes


def mxq(x, axis, fmt="e4m3"):
    dtype, down = {"e4m3": (ml_dtypes.float8_e4m3fn, 7), "e5m2": (ml_dtypes.float8_e5m2, 14)}[fmt]
    v = np.moveaxis(np.asarray(x, np.float32).astype(ml_dtypes.bfloat16).astype(np.float64), axis, -1)
    blocks = v.reshape(v.shape[:-1] + (-1, 32))
    amax = np.abs(blocks).max(-1, keepdims=True)
    byte = np.maximum(np.where(amax > 0, np.frexp(amax)[1] - 1 + 127, 0) - down, 1)
    scale = np.exp2(byte - 127.0)
    codes = (blocks / scale).astype(np.float32).astype(dtype).astype(np.float64)
    return np.moveaxis((codes * scale).reshape(v.shape), -1, axis)


WIDE = False


def mx_kscale(k):
    if not WIDE:
        return np.ones(k)
    levels = np.array([10, -10, 5, -5, 0])
    a = np.random.permutation(np.resize(levels, k // 512 * 4)).reshape(k // 512, 4)
    idx = np.arange(k)
    return np.exp2(a[idx // 512, idx % 128 // 32])


BF16 = ml_dtypes.bfloat16


def bf(x):
    return np.asarray(x, np.float32).astype(BF16)


def f64(x):
    return np.asarray(x).astype(np.float64)


E2M1 = np.array([0.0, 0.5, 1.0, 1.5, 2.0, 3.0, 4.0, 6.0, -0.0, -0.5, -1.0, -1.5, -2.0, -3.0, -4.0, -6.0])


def pack_weight(w, fmt):
    k, n = w.shape
    w = f64(bf(w)).reshape(k // 32, 32, n)
    amax = np.abs(w).max(1)
    if fmt == "e4m3":
        byte = np.frexp(amax)[1] - 1 + 127 - 7
    else:
        mant, ex = np.frexp(amax / 6.0)
        byte = np.where(mant > 0.5, ex, ex - 1) + 127
    byte = np.clip(np.where(amax > 0, byte, 1), 1, 254)
    scaled = (w * np.exp2(127.0 - byte)[:, None, :]).reshape(k, n).astype(np.float32)
    by_word = np.ascontiguousarray(scaled.reshape(k // 512, 128, 4, n).transpose(0, 1, 3, 2))
    if fmt == "e4m3":
        words = by_word.astype(ml_dtypes.float8_e4m3fn).view(np.uint8)
    else:
        c = by_word.astype(ml_dtypes.float4_e2m1fn).view(np.uint8) & 0xF
        words = c[..., 0::2] | (c[..., 1::2] << 4)
    return np.ascontiguousarray(words), np.ascontiguousarray(byte.astype(np.uint8).reshape(k // 512, 16, n))


def unpack_weight(words, scales, fmt):
    g, p, n, _ = words.shape
    if fmt == "e4m3":
        vals = np.ascontiguousarray(words).view(ml_dtypes.float8_e4m3fn).astype(np.float64)
    else:
        nib = np.empty((g, p, n, 4), np.uint8)
        nib[..., 0::2] = words & 0xF
        nib[..., 1::2] = words >> 4
        vals = E2M1[nib]
    vals = vals * np.repeat(np.exp2(scales.astype(np.float64) - 127.0), 8, axis=1)[..., None]
    return vals.transpose(0, 1, 3, 2).reshape(g * 512, n)


E, T, H, D, R = 4, 256, 1024, 1024, 128
SCALE = 2.0


def setup_inputs():
    s = mx_kscale(D)
    h = bf(np.random.standard_normal((E, T, D)) * 0.8 * s)
    low_d = bf(np.random.standard_normal((E, T, R)) * 1.2)
    W_d = np.random.standard_normal((E, H, D)) * 1.5 / np.sqrt(D) / s
    B_d = bf(np.random.standard_normal((E, H, R)) * 0.3 / np.sqrt(R))
    cat = np.ascontiguousarray(W_d.swapaxes(1, 2)).reshape(-1, H)
    words, scales = pack_weight(cat, "e4m3")
    return {"h": h,
            "low_d": low_d,
            "W_d_words": words,
            "W_d_scales": scales,
            "B_d": B_d}


def reference(h, low_d, W_d_words, W_d_scales, B_d):
    base = mxq(f64(h), 2, "e4m3") @ unpack_weight(W_d_words, W_d_scales, "e4m3").reshape(E, D, H)
    delta = f64(low_d) @ f64(B_d).transpose(0, 2, 1)
    out = base + SCALE * delta
    return out.reshape(-1, H)

@@ -1,0 +1,190 @@
+from contextlib import ExitStack
+
+import concourse.mybir as mybir
+from concourse.masks import make_identity
+
+F32 = mybir.dt.float32
+BF16 = mybir.dt.bfloat16
+I32 = mybir.dt.int32
+U32 = mybir.dt.uint32
+U8 = mybir.dt.uint8
+FP8X4 = mybir.dt.float8_e4m3fn_x4
+ADD = mybir.AluOpType.add
+
+E, T, H, D, R = 4, 256, 1024, 1024, 128
+LORA_SCALE = 2.0
+
+P = 128
+PACK = 4
+K_PASS = P * PACK
+PASSES = D // K_PASS
+TOK_TILES = T // P
+N_TILE = 512
+N_TILES = H // N_TILE
+B_BLOCKS = H // P
+WORDS = K_PASS // 2
+PLANES_PER_TILE = 4
+
+FLOPS = 2 * E * T * D * H + 2 * E * T * R * H
+
+
+def tile_loralinearexpertswrapper_pb_e_kernel(tc, h, low_d, W_d_words, W_d_scales, B_d, out):
+    nc = tc.nc
+
+    h_view = h.rearrange("e (p j) k -> e p j k", j=TOK_TILES)
+    low_view = low_d.rearrange("e (p j) r -> p e (j r)", j=TOK_TILES)
+    out_view = out.rearrange("(e p j) n -> e p j n", p=P, j=TOK_TILES)
+    b_view = B_d.rearrange("e (p c) r -> e p (c r)", c=B_BLOCKS)
+
+    with ExitStack() as ctx:
+        ctx.enter_context(tc.manual_schedule())
+        keep = ctx.enter_context(tc.tile_pool(name="keep", bufs=1))
+        psum_t = ctx.enter_context(tc.psum_pool(name="psum_t", bufs=3))
+        psum_d = ctx.enter_context(tc.psum_pool(name="psum_d", bufs=2))
+        psum_m = ctx.enter_context(tc.psum_pool(name="psum_m", bufs=3))
+
+        h_sb = [keep.tile([P, TOK_TILES, D], BF16, name="h_sb%d" % e) for e in range(E)]
+        b_sb = [keep.tile([P, B_BLOCKS, R], BF16, name="b_sb%d" % e) for e in range(E)]
+        low_sb = keep.tile([P, E, TOK_TILES * R], BF16, name="low_sb")
+        w_words = [keep.tile([P, PASSES, H], U32, name="w_words%d" % e, align_bytes=64) for e in range(E)]
+        w_planes = keep.tile([P, (E * PASSES // PLANES_PER_TILE) * H], U8, name="w_planes", align_bytes=64)
+        grouped = [keep.tile([P, PASSES, T, PACK], BF16, name="grouped%d" % e, align_bytes=64) for e in range(E)]
+        h_codes = [keep.tile([P, PASSES * T], U32, name="h_codes%d" % e, align_bytes=64) for e in range(E)]
+        h_scales = [keep.tile([P, PASSES * T], U8, name="h_scales%d" % e, align_bytes=64) for e in range(E)]
+        lowT_sb = keep.tile([P, E * TOK_TILES, P], BF16, name="lowT_sb")
+        bT_sb = [keep.tile([P, H], BF16, name="bT_sb%d" % e) for e in range(E)]
+        out_sb = [keep.tile([P, TOK_TILES, H], F32, name="out_sb%d" % e) for e in range(E)]
+        ident_f32 = keep.tile([P, P], F32, name="ident_f32")
+        ident_bf16 = keep.tile([P, P], BF16, name="ident_bf16")
+
+        nc.vector.memset(w_planes[:].bitcast(I32), 0)
+        make_identity(nc, ident_bf16[:])
+        make_identity(nc, ident_f32[:])
+
+        def load_lora_weight(e):
+            nc.sync.dma_start(out=b_sb[e][:].rearrange("p c r -> p (c r)"), in_=b_view[e])
+
+        def load_h(e):
+            nc.sync.dma_start(out=h_sb[e][:], in_=h_view[e])
+
+        def load_weight(e):
+            nc.sync.dma_start(
+                out=w_words[e][:].bitcast(I32),
+                in_=W_d_words[PASSES * e : PASSES * (e + 1)].rearrange("g p n t -> p g (n t)").bitcast(I32),
+            )
+
+        def load_scale_planes(a):
+            for quadrant in range(4):
+                nc.sync.dma_start(
+                    out=w_planes[32 * quadrant : 32 * quadrant + 16, a * H : (a + 1) * H].bitcast(I32),
+                    in_=W_d_scales[
+                        PLANES_PER_TILE * a : PLANES_PER_TILE * (a + 1), 4 * quadrant : 4 * quadrant + 4, :
+                    ].bitcast(I32),
+                )
+
+        load_lora_weight(0)
+        nc.sync.dma_start(out=low_sb[:], in_=low_view)
+        load_h(0)
+        load_scale_planes(0)
+        load_lora_weight(1)
+        load_h(1)
+        load_weight(0)
+        load_lora_weight(2)
+        load_h(2)
+        load_weight(1)
+        load_scale_planes(1)
+        load_lora_weight(3)
+        load_h(3)
+        load_weight(2)
+        load_weight(3)
+
+        def transpose_lora_weight(e):
+            bT_ps = psum_t.tile([P, B_BLOCKS, P], BF16, name="bT_ps", tag="t")
+            for c in range(B_BLOCKS):
+                nc.tensor.transpose(bT_ps[:, c, :], b_sb[e][:, c, :], ident_bf16[:])
+            nc.scalar.copy(
+                out=bT_sb[e][:].rearrange("r (p c) -> r p c", c=B_BLOCKS),
+                in_=bT_ps[:].rearrange("r c p -> r p c"),
+            )
+
+        def transpose_low():
+            lowT_ps = psum_t.tile([P, E * TOK_TILES, P], BF16, name="lowT_ps", tag="t")
+            for e in range(E):
+                for j in range(TOK_TILES):
+                    nc.tensor.transpose(
+                        lowT_ps[:, TOK_TILES * e + j, :], low_sb[:, e, j * R : (j + 1) * R], ident_bf16[:]
+                    )
+            nc.scalar.copy(out=lowT_sb[:], in_=lowT_ps[:])
+
+        def transpose_h(e):
+            for g in range(PASSES):
+                hT_ps = psum_t.tile([P, 2, T], F32, name="hT_ps", tag="t")
+                for j in range(TOK_TILES):
+                    h_pairs = h_sb[e][:, j, :].bitcast(F32)
+                    for u in range(2):
+                        nc.tensor.transpose(
+                            hT_ps[:, u, j * P : (j + 1) * P],
+                            h_pairs[:, WORDS * g + u : WORDS * (g + 1) : 2],
+                            ident_f32[:],
+                        )
+                pairs_out = grouped[e][:, g].rearrange("p m t -> p (m t)").bitcast(F32)
+                copy = nc.vector.tensor_copy if g == 0 else nc.scalar.copy
+                copy(out=pairs_out.rearrange("p (m u) -> p m u", u=2), in_=hT_ps[:].rearrange("p u m -> p m u"))
+
+        def quantise_h(e):
+            nc.vector.quantize_mx(
+                out=h_codes[e][:].bitcast(FP8X4),
+                scales=h_scales[e][:],
+                in_=grouped[e][:].rearrange("p g m t -> p (g m t)"),
+            )
+
+        def lora_product(e, j, n):
+            n_cols = slice(n * N_TILE, (n + 1) * N_TILE)
+            delta = psum_d.tile([P, N_TILE], F32, name="delta")
+            nc.tensor.matmul(
+                delta[:], lhsT=lowT_sb[:, TOK_TILES * e + j, :], rhs=bT_sb[e][:, n_cols], start=True, stop=True
+            )
+            nc.scalar.mul(out_sb[e][:, j, n_cols], delta[:], LORA_SCALE)
+
+        def mx_product(e, j, n):
+            n_cols = slice(n * N_TILE, (n + 1) * N_TILE)
+            acc = psum_m.tile([P, N_TILE], F32, name="acc")
+            for g in range(PASSES):
+                g_cat = PASSES * e + g
+                first_row = 4 * (g_cat % PLANES_PER_TILE)
+                first_col = (g_cat // PLANES_PER_TILE) * H + n * N_TILE
+                tokens = slice(g * T + j * P, g * T + (j + 1) * P)
+                nc.tensor.matmul_mx(
+                    out=acc[:],
+                    lhsT=h_codes[e][:, tokens].bitcast(FP8X4),
+                    lhsT_scale=h_scales[e][:, tokens],
+                    rhs=w_words[e][:, g, n_cols].bitcast(FP8X4),
+                    rhs_scale=w_planes[first_row:P, first_col : first_col + N_TILE],
+                    start=(g == 0),
+                    stop=(g == PASSES - 1),
+                )
+            nc.vector.tensor_tensor(out=out_sb[e][:, j, n_cols], in0=acc[:], in1=out_sb[e][:, j, n_cols], op=ADD)
+
+        def prepare(e):
+            transpose_lora_weight(e)
+            transpose_h(e)
+            quantise_h(e)
+
+        banks = [(j, n) for j in range(TOK_TILES) for n in range(N_TILES)]
+
+        transpose_lora_weight(0)
+        transpose_low()
+        transpose_h(0)
+        quantise_h(0)
+        for j, n in banks:
+            lora_product(0, j, n)
+        prepare(1)
+        for e in range(E):
+            for j, n in banks:
+                mx_product(e, j, n)
+                if e + 1 < E:
+                    lora_product(e + 1, j, n)
+                if n == N_TILES - 1:
+                    nc.sync.dma_start(out=out_view[e][:, j, :], in_=out_sb[e][:, j, :])
+            if e + 2 < E:
+                prepare(e + 2)

@@ -23,6 +23,7 @@ N_TILE = 512
 N_TILES = H // N_TILE
 B_BLOCKS = H // P
 WORDS = K_PASS // 2
+PSUM_BANKS = 8
 PLANES_PER_TILE = 4
 
 FLOPS = 2 * E * T * D * H + 2 * E * T * R * H
@@ -39,9 +40,7 @@ def tile_loralinearexpertswrapper_pb_e_kernel(tc, h, low_d, W_d_words, W_d_scale
     with ExitStack() as ctx:
         ctx.enter_context(tc.manual_schedule())
         keep = ctx.enter_context(tc.tile_pool(name="keep", bufs=1))
-        psum_t = ctx.enter_context(tc.psum_pool(name="psum_t", bufs=3))
-        psum_d = ctx.enter_context(tc.psum_pool(name="psum_d", bufs=2))
-        psum_m = ctx.enter_context(tc.psum_pool(name="psum_m", bufs=3))
+        psum = ctx.enter_context(tc.psum_pool(name="psum", bufs=PSUM_BANKS))
 
         h_sb = [keep.tile([P, TOK_TILES, D], BF16, name="h_sb%d" % e) for e in range(E)]
         b_sb = [keep.tile([P, B_BLOCKS, R], BF16, name="b_sb%d" % e) for e in range(E)]
@@ -75,40 +74,37 @@ def tile_loralinearexpertswrapper_pb_e_kernel(tc, h, low_d, W_d_words, W_d_scale
 
         def load_scale_planes(a):
             for quadrant in range(4):
-                nc.sync.dma_start(
-                    out=w_planes[32 * quadrant : 32 * quadrant + 16, a * H : (a + 1) * H].bitcast(I32),
+                nc.gpsimd.dma_start(
+                    out=w_planes[32 * quadrant : 32 * quadrant + 16, a * H : (a + 1) * H].bitcast(F32),
                     in_=W_d_scales[
                         PLANES_PER_TILE * a : PLANES_PER_TILE * (a + 1), 4 * quadrant : 4 * quadrant + 4, :
-                    ].bitcast(I32),
+                    ].bitcast(F32),
                 )
 
+        load_scale_planes(0)
+        load_scale_planes(1)
         load_lora_weight(0)
         nc.sync.dma_start(out=low_sb[:], in_=low_view)
+        for e in range(1, E):
+            load_lora_weight(e)
         load_h(0)
-        load_scale_planes(0)
-        load_lora_weight(1)
-        load_h(1)
-        load_weight(0)
-        load_lora_weight(2)
-        load_h(2)
-        load_weight(1)
-        load_scale_planes(1)
-        load_lora_weight(3)
-        load_h(3)
-        load_weight(2)
-        load_weight(3)
+        for e in range(E):
+            if e + 1 < E:
+                load_h(e + 1)
+            load_weight(e)
 
         def transpose_lora_weight(e):
-            bT_ps = psum_t.tile([P, B_BLOCKS, P], BF16, name="bT_ps", tag="t")
+            bT_ps = psum.tile([P, B_BLOCKS, P], BF16, name="bT_ps", tag="bank")
             for c in range(B_BLOCKS):
                 nc.tensor.transpose(bT_ps[:, c, :], b_sb[e][:, c, :], ident_bf16[:])
-            nc.scalar.copy(
+            copy = nc.scalar.copy if e % 2 == 0 else nc.vector.tensor_copy
+            copy(
                 out=bT_sb[e][:].rearrange("r (p c) -> r p c", c=B_BLOCKS),
                 in_=bT_ps[:].rearrange("r c p -> r p c"),
             )
 
         def transpose_low():
-            lowT_ps = psum_t.tile([P, E * TOK_TILES, P], BF16, name="lowT_ps", tag="t")
+            lowT_ps = psum.tile([P, E * TOK_TILES, P], BF16, name="lowT_ps", tag="bank")
             for e in range(E):
                 for j in range(TOK_TILES):
                     nc.tensor.transpose(
@@ -118,7 +114,7 @@ def tile_loralinearexpertswrapper_pb_e_kernel(tc, h, low_d, W_d_words, W_d_scale
 
         def transpose_h(e):
             for g in range(PASSES):
-                hT_ps = psum_t.tile([P, 2, T], F32, name="hT_ps", tag="t")
+                hT_ps = psum.tile([P, 2, T], F32, name="hT_ps", tag="bank")
                 for j in range(TOK_TILES):
                     h_pairs = h_sb[e][:, j, :].bitcast(F32)
                     for u in range(2):
@@ -128,8 +124,9 @@ def tile_loralinearexpertswrapper_pb_e_kernel(tc, h, low_d, W_d_words, W_d_scale
                             ident_f32[:],
                         )
                 pairs_out = grouped[e][:, g].rearrange("p m t -> p (m t)").bitcast(F32)
-                copy = nc.vector.tensor_copy if g == 0 else nc.scalar.copy
-                copy(out=pairs_out.rearrange("p (m u) -> p m u", u=2), in_=hT_ps[:].rearrange("p u m -> p m u"))
+                nc.scalar.copy(
+                    out=pairs_out.rearrange("p (m u) -> p m u", u=2), in_=hT_ps[:].rearrange("p u m -> p m u")
+                )
 
         def quantise_h(e):
             nc.vector.quantize_mx(
@@ -140,15 +137,18 @@ def tile_loralinearexpertswrapper_pb_e_kernel(tc, h, low_d, W_d_words, W_d_scale
 
         def lora_product(e, j, n):
             n_cols = slice(n * N_TILE, (n + 1) * N_TILE)
-            delta = psum_d.tile([P, N_TILE], F32, name="delta")
+            delta = psum.tile([P, N_TILE], F32, name="delta", tag="bank")
             nc.tensor.matmul(
                 delta[:], lhsT=lowT_sb[:, TOK_TILES * e + j, :], rhs=bT_sb[e][:, n_cols], start=True, stop=True
             )
-            nc.scalar.mul(out_sb[e][:, j, n_cols], delta[:], LORA_SCALE)
+            if n == 0:
+                nc.scalar.mul(out_sb[e][:, j, n_cols], delta[:], LORA_SCALE)
+            else:
+                nc.vector.tensor_scalar_mul(out_sb[e][:, j, n_cols], delta[:], LORA_SCALE)
 
         def mx_product(e, j, n):
             n_cols = slice(n * N_TILE, (n + 1) * N_TILE)
-            acc = psum_m.tile([P, N_TILE], F32, name="acc")
+            acc = psum.tile([P, N_TILE], F32, name="acc", tag="bank")
             for g in range(PASSES):
                 g_cat = PASSES * e + g
                 first_row = 4 * (g_cat % PLANES_PER_TILE)
@@ -165,26 +165,26 @@ def tile_loralinearexpertswrapper_pb_e_kernel(tc, h, low_d, W_d_words, W_d_scale
                 )
             nc.vector.tensor_tensor(out=out_sb[e][:, j, n_cols], in0=acc[:], in1=out_sb[e][:, j, n_cols], op=ADD)
 
-        def prepare(e):
-            transpose_lora_weight(e)
-            transpose_h(e)
-            quantise_h(e)
-
-        banks = [(j, n) for j in range(TOK_TILES) for n in range(N_TILES)]
+        def lora_products(e):
+            for j in range(TOK_TILES):
+                for n in range(N_TILES):
+                    lora_product(e, j, n)
 
         transpose_lora_weight(0)
         transpose_low()
+        for e in range(1, E):
+            transpose_lora_weight(e)
+            lora_products(e - 1)
         transpose_h(0)
         quantise_h(0)
-        for j, n in banks:
-            lora_product(0, j, n)
-        prepare(1)
+        lora_products(E - 1)
+        transpose_h(1)
         for e in range(E):
-            for j, n in banks:
-                mx_product(e, j, n)
-                if e + 1 < E:
-                    lora_product(e + 1, j, n)
-                if n == N_TILES - 1:
-                    nc.sync.dma_start(out=out_view[e][:, j, :], in_=out_sb[e][:, j, :])
+            for j in range(TOK_TILES):
+                for n in range(N_TILES):
+                    mx_product(e, j, n)
+                nc.sync.dma_start(out=out_view[e][:, j, :], in_=out_sb[e][:, j, :])
+                if j == 0 and e + 1 < E:
+                    quantise_h(e + 1)
             if e + 2 < E:
-                prepare(e + 2)
+                transpose_h(e + 2)

@@ -74,15 +74,13 @@ def tile_loralinearexpertswrapper_pb_e_kernel(tc, h, low_d, W_d_words, W_d_scale
 
         def load_scale_planes(a):
             for quadrant in range(4):
-                nc.gpsimd.dma_start(
-                    out=w_planes[32 * quadrant : 32 * quadrant + 16, a * H : (a + 1) * H].bitcast(F32),
+                nc.sync.dma_start(
+                    out=w_planes[32 * quadrant : 32 * quadrant + 16, a * H : (a + 1) * H].bitcast(I32),
                     in_=W_d_scales[
                         PLANES_PER_TILE * a : PLANES_PER_TILE * (a + 1), 4 * quadrant : 4 * quadrant + 4, :
-                    ].bitcast(F32),
+                    ].bitcast(I32),
                 )
 
-        load_scale_planes(0)
-        load_scale_planes(1)
         load_lora_weight(0)
         nc.sync.dma_start(out=low_sb[:], in_=low_view)
         for e in range(1, E):
@@ -91,6 +89,8 @@ def tile_loralinearexpertswrapper_pb_e_kernel(tc, h, low_d, W_d_words, W_d_scale
         for e in range(E):
             if e + 1 < E:
                 load_h(e + 1)
+            if e % 2 == 0:
+                load_scale_planes(e // 2)
             load_weight(e)
 
         def transpose_lora_weight(e):
@@ -110,7 +110,7 @@ def tile_loralinearexpertswrapper_pb_e_kernel(tc, h, low_d, W_d_words, W_d_scale
                     nc.tensor.transpose(
                         lowT_ps[:, TOK_TILES * e + j, :], low_sb[:, e, j * R : (j + 1) * R], ident_bf16[:]
                     )
-            nc.scalar.copy(out=lowT_sb[:], in_=lowT_ps[:])
+            nc.vector.tensor_copy(out=lowT_sb[:], in_=lowT_ps[:])
 
         def transpose_h(e):
             for g in range(PASSES):
@@ -165,6 +165,9 @@ def tile_loralinearexpertswrapper_pb_e_kernel(tc, h, low_d, W_d_words, W_d_scale
                 )
             nc.vector.tensor_tensor(out=out_sb[e][:, j, n_cols], in0=acc[:], in1=out_sb[e][:, j, n_cols], op=ADD)
 
+        def store(e, j, cols):
+            nc.sync.dma_start(out=out_view[e][:, j, cols], in_=out_sb[e][:, j, cols])
+
         def lora_products(e):
             for j in range(TOK_TILES):
                 for n in range(N_TILES):
@@ -181,9 +184,13 @@ def tile_loralinearexpertswrapper_pb_e_kernel(tc, h, low_d, W_d_words, W_d_scale
         transpose_h(1)
         for e in range(E):
             for j in range(TOK_TILES):
+                last_tile = e == E - 1 and j == TOK_TILES - 1
                 for n in range(N_TILES):
                     mx_product(e, j, n)
-                nc.sync.dma_start(out=out_view[e][:, j, :], in_=out_sb[e][:, j, :])
+                    if last_tile:
+                        store(e, j, slice(n * N_TILE, (n + 1) * N_TILE))
+                if not last_tile:
+                    store(e, j, slice(0, H))
                 if j == 0 and e + 1 < E:
                     quantise_h(e + 1)
             if e + 2 < E:

@@ -83,21 +83,25 @@ def tile_loralinearexpertswrapper_pb_e_kernel(tc, h, low_d, W_d_words, W_d_scale
 
         load_lora_weight(0)
         nc.sync.dma_start(out=low_sb[:], in_=low_view)
-        for e in range(1, E):
-            load_lora_weight(e)
+        load_lora_weight(1)
         load_h(0)
-        for e in range(E):
-            if e + 1 < E:
-                load_h(e + 1)
-            if e % 2 == 0:
-                load_scale_planes(e // 2)
-            load_weight(e)
+        load_lora_weight(2)
+        load_h(1)
+        load_scale_planes(0)
+        load_weight(0)
+        load_lora_weight(3)
+        load_h(2)
+        load_weight(1)
+        load_h(3)
+        load_scale_planes(1)
+        load_weight(2)
+        load_weight(3)
 
         def transpose_lora_weight(e):
             bT_ps = psum.tile([P, B_BLOCKS, P], BF16, name="bT_ps", tag="bank")
             for c in range(B_BLOCKS):
                 nc.tensor.transpose(bT_ps[:, c, :], b_sb[e][:, c, :], ident_bf16[:])
-            copy = nc.scalar.copy if e % 2 == 0 else nc.vector.tensor_copy
+            copy = nc.vector.tensor_copy if e == 1 else nc.scalar.copy
             copy(
                 out=bT_sb[e][:].rearrange("r (p c) -> r p c", c=B_BLOCKS),
                 in_=bT_ps[:].rearrange("r c p -> r p c"),
@@ -141,7 +145,7 @@ def tile_loralinearexpertswrapper_pb_e_kernel(tc, h, low_d, W_d_words, W_d_scale
             nc.tensor.matmul(
                 delta[:], lhsT=lowT_sb[:, TOK_TILES * e + j, :], rhs=bT_sb[e][:, n_cols], start=True, stop=True
             )
-            if n == 0:
+            if n == 0 or e >= 2:
                 nc.scalar.mul(out_sb[e][:, j, n_cols], delta[:], LORA_SCALE)
             else:
                 nc.vector.tensor_scalar_mul(out_sb[e][:, j, n_cols], delta[:], LORA_SCALE)
@@ -173,16 +177,7 @@ def tile_loralinearexpertswrapper_pb_e_kernel(tc, h, low_d, W_d_words, W_d_scale
                 for n in range(N_TILES):
                     lora_product(e, j, n)
 
-        transpose_lora_weight(0)
-        transpose_low()
-        for e in range(1, E):
-            transpose_lora_weight(e)
-            lora_products(e - 1)
-        transpose_h(0)
-        quantise_h(0)
-        lora_products(E - 1)
-        transpose_h(1)
-        for e in range(E):
+        def mx_products(e):
             for j in range(TOK_TILES):
                 last_tile = e == E - 1 and j == TOK_TILES - 1
                 for n in range(N_TILES):
@@ -191,7 +186,25 @@ def tile_loralinearexpertswrapper_pb_e_kernel(tc, h, low_d, W_d_words, W_d_scale
                         store(e, j, slice(n * N_TILE, (n + 1) * N_TILE))
                 if not last_tile:
                     store(e, j, slice(0, H))
-                if j == 0 and e + 1 < E:
-                    quantise_h(e + 1)
-            if e + 2 < E:
-                transpose_h(e + 2)
+
+        transpose_lora_weight(0)
+        transpose_low()
+        transpose_lora_weight(1)
+        lora_products(0)
+        transpose_h(0)
+        transpose_lora_weight(2)
+        quantise_h(0)
+        lora_products(1)
+        transpose_h(1)
+        quantise_h(1)
+        mx_products(0)
+        transpose_lora_weight(3)
+        transpose_h(2)
+        lora_products(2)
+        quantise_h(2)
+        mx_products(1)
+        transpose_h(3)
+        lora_products(3)
+        quantise_h(3)
+        mx_products(2)
+        mx_products(3)

@@ -24,6 +24,9 @@ N_TILES = H // N_TILE
 B_BLOCKS = H // P
 WORDS = K_PASS // 2
 PSUM_BANKS = 8
+LOW_BLOCKS = E * T // P
+LOW_ROWS = P // E
+WHOLE_STORES = 2
 PLANES_PER_TILE = 4
 
 FLOPS = 2 * E * T * D * H + 2 * E * T * R * H
@@ -33,7 +36,7 @@ def tile_loralinearexpertswrapper_pb_e_kernel(tc, h, low_d, W_d_words, W_d_scale
     nc = tc.nc
 
     h_view = h.rearrange("e (p j) k -> e p j k", j=TOK_TILES)
-    low_view = low_d.rearrange("e (p j) r -> p e (j r)", j=TOK_TILES)
+    low_view = low_d.rearrange("e t r -> (e t) r").rearrange("(p c) r -> p (c r)", c=LOW_BLOCKS)
     out_view = out.rearrange("(e p j) n -> e p j n", p=P, j=TOK_TILES)
     b_view = B_d.rearrange("e (p c) r -> e p (c r)", c=B_BLOCKS)
 
@@ -44,13 +47,14 @@ def tile_loralinearexpertswrapper_pb_e_kernel(tc, h, low_d, W_d_words, W_d_scale
 
         h_sb = [keep.tile([P, TOK_TILES, D], BF16, name="h_sb%d" % e) for e in range(E)]
         b_sb = [keep.tile([P, B_BLOCKS, R], BF16, name="b_sb%d" % e) for e in range(E)]
-        low_sb = keep.tile([P, E, TOK_TILES * R], BF16, name="low_sb")
+        low_sb = keep.tile([P, LOW_BLOCKS, R], BF16, name="low_sb")
         w_words = [keep.tile([P, PASSES, H], U32, name="w_words%d" % e, align_bytes=64) for e in range(E)]
         w_planes = keep.tile([P, (E * PASSES // PLANES_PER_TILE) * H], U8, name="w_planes", align_bytes=64)
         grouped = [keep.tile([P, PASSES, T, PACK], BF16, name="grouped%d" % e, align_bytes=64) for e in range(E)]
         h_codes = [keep.tile([P, PASSES * T], U32, name="h_codes%d" % e, align_bytes=64) for e in range(E)]
         h_scales = [keep.tile([P, PASSES * T], U8, name="h_scales%d" % e, align_bytes=64) for e in range(E)]
-        lowT_sb = keep.tile([P, E * TOK_TILES, P], BF16, name="lowT_sb")
+        lowT_first = keep.tile([P, TOK_TILES, LOW_ROWS, LOW_BLOCKS // TOK_TILES], BF16, name="lowT_first")
+        lowT_sb = keep.tile([P, TOK_TILES, P - LOW_ROWS, LOW_BLOCKS // TOK_TILES], BF16, name="lowT_sb")
         bT_sb = [keep.tile([P, H], BF16, name="bT_sb%d" % e) for e in range(E)]
         out_sb = [keep.tile([P, TOK_TILES, H], F32, name="out_sb%d" % e) for e in range(E)]
         ident_f32 = keep.tile([P, P], F32, name="ident_f32")
@@ -82,7 +86,7 @@ def tile_loralinearexpertswrapper_pb_e_kernel(tc, h, low_d, W_d_words, W_d_scale
                 )
 
         load_lora_weight(0)
-        nc.sync.dma_start(out=low_sb[:], in_=low_view)
+        nc.sync.dma_start(out=low_sb[:].rearrange("p c r -> p (c r)"), in_=low_view)
         load_lora_weight(1)
         load_h(0)
         load_lora_weight(2)
@@ -108,13 +112,12 @@ def tile_loralinearexpertswrapper_pb_e_kernel(tc, h, low_d, W_d_words, W_d_scale
             )
 
         def transpose_low():
-            lowT_ps = psum.tile([P, E * TOK_TILES, P], BF16, name="lowT_ps", tag="bank")
-            for e in range(E):
-                for j in range(TOK_TILES):
-                    nc.tensor.transpose(
-                        lowT_ps[:, TOK_TILES * e + j, :], low_sb[:, e, j * R : (j + 1) * R], ident_bf16[:]
-                    )
-            nc.vector.tensor_copy(out=lowT_sb[:], in_=lowT_ps[:])
+            lowT_ps = psum.tile([P, LOW_BLOCKS, P], BF16, name="lowT_ps", tag="bank")
+            for c in range(LOW_BLOCKS):
+                nc.tensor.transpose(lowT_ps[:, c, :], low_sb[:, c, :], ident_bf16[:])
+            sorted_view = lowT_ps[:].rearrange("r (b j) p -> r j p b", j=TOK_TILES)
+            nc.vector.tensor_copy(out=lowT_first[:], in_=sorted_view[:, :, 0:LOW_ROWS, :])
+            nc.vector.tensor_copy(out=lowT_sb[:], in_=sorted_view[:, :, LOW_ROWS:P, :])
 
         def transpose_h(e):
             for g in range(PASSES):
@@ -143,7 +146,13 @@ def tile_loralinearexpertswrapper_pb_e_kernel(tc, h, low_d, W_d_words, W_d_scale
             n_cols = slice(n * N_TILE, (n + 1) * N_TILE)
             delta = psum.tile([P, N_TILE], F32, name="delta", tag="bank")
             nc.tensor.matmul(
-                delta[:], lhsT=lowT_sb[:, TOK_TILES * e + j, :], rhs=bT_sb[e][:, n_cols], start=True, stop=True
+                delta[:],
+                lhsT=(
+                    lowT_first[:, j, :, :] if e == 0 else lowT_sb[:, j, LOW_ROWS * (e - 1) : LOW_ROWS * e, :]
+                ).rearrange("r a b -> r (a b)"),
+                rhs=bT_sb[e][:, n_cols],
+                start=True,
+                stop=True,
             )
             if n == 0 or e >= 2:
                 nc.scalar.mul(out_sb[e][:, j, n_cols], delta[:], LORA_SCALE)
@@ -172,6 +181,11 @@ def tile_loralinearexpertswrapper_pb_e_kernel(tc, h, low_d, W_d_words, W_d_scale
         def store(e, j, cols):
             nc.sync.dma_start(out=out_view[e][:, j, cols], in_=out_sb[e][:, j, cols])
 
+        def store_expert(e):
+            nc.sync.dma_start(
+                out=out_view[e].rearrange("p j n -> p (j n)"), in_=out_sb[e][:].rearrange("p j n -> p (j n)")
+            )
+
         def lora_products(e):
             for j in range(TOK_TILES):
                 for n in range(N_TILES):
@@ -184,8 +198,10 @@ def tile_loralinearexpertswrapper_pb_e_kernel(tc, h, low_d, W_d_words, W_d_scale
                     mx_product(e, j, n)
                     if last_tile:
                         store(e, j, slice(n * N_TILE, (n + 1) * N_TILE))
-                if not last_tile:
+                if e >= WHOLE_STORES and not last_tile:
                     store(e, j, slice(0, H))
+            if e < WHOLE_STORES:
+                store_expert(e)
 
         transpose_lora_weight(0)
         transpose_low()

@@ -91,8 +91,8 @@ def tile_loralinearexpertswrapper_pb_e_kernel(tc, h, low_d, W_d_words, W_d_scale
         load_h(0)
         load_lora_weight(2)
         load_h(1)
-        load_scale_planes(0)
         load_weight(0)
+        load_scale_planes(0)
         load_lora_weight(3)
         load_h(2)
         load_weight(1)
@@ -193,12 +193,9 @@ def tile_loralinearexpertswrapper_pb_e_kernel(tc, h, low_d, W_d_words, W_d_scale
 
         def mx_products(e):
             for j in range(TOK_TILES):
-                last_tile = e == E - 1 and j == TOK_TILES - 1
                 for n in range(N_TILES):
                     mx_product(e, j, n)
-                    if last_tile:
-                        store(e, j, slice(n * N_TILE, (n + 1) * N_TILE))
-                if e >= WHOLE_STORES and not last_tile:
+                if e >= WHOLE_STORES:
                     store(e, j, slice(0, H))
             if e < WHOLE_STORES:
                 store_expert(e)

from contextlib import ExitStack

import concourse.mybir as mybir
from concourse.masks import make_identity

F32 = mybir.dt.float32
BF16 = mybir.dt.bfloat16
I32 = mybir.dt.int32
U32 = mybir.dt.uint32
U8 = mybir.dt.uint8
FP8X4 = mybir.dt.float8_e4m3fn_x4
ADD = mybir.AluOpType.add

E, T, H, D, R = 4, 256, 1024, 1024, 128
LORA_SCALE = 2.0

P = 128
PACK = 4
K_PASS = P * PACK
PASSES = D // K_PASS
TOK_TILES = T // P
N_TILE = 512
N_TILES = H // N_TILE
B_BLOCKS = H // P
WORDS = K_PASS // 2
PSUM_BANKS = 8
LOW_BLOCKS = E * T // P
LOW_ROWS = P // E
WHOLE_STORES = 2
PLANES_PER_TILE = 4

FLOPS = 2 * E * T * D * H + 2 * E * T * R * H


def tile_loralinearexpertswrapper_pb_e_kernel(tc, h, low_d, W_d_words, W_d_scales, B_d, out):
    nc = tc.nc

    h_view = h.rearrange("e (p j) k -> e p j k", j=TOK_TILES)
    low_view = low_d.rearrange("e t r -> (e t) r").rearrange("(p c) r -> p (c r)", c=LOW_BLOCKS)
    out_view = out.rearrange("(e p j) n -> e p j n", p=P, j=TOK_TILES)
    b_view = B_d.rearrange("e (p c) r -> e p (c r)", c=B_BLOCKS)

    with ExitStack() as ctx:
        ctx.enter_context(tc.manual_schedule())
        keep = ctx.enter_context(tc.tile_pool(name="keep", bufs=1))
        psum = ctx.enter_context(tc.psum_pool(name="psum", bufs=PSUM_BANKS))

        h_sb = [keep.tile([P, TOK_TILES, D], BF16, name="h_sb%d" % e) for e in range(E)]
        b_sb = [keep.tile([P, B_BLOCKS, R], BF16, name="b_sb%d" % e) for e in range(E)]
        low_sb = keep.tile([P, LOW_BLOCKS, R], BF16, name="low_sb")
        w_words = [keep.tile([P, PASSES, H], U32, name="w_words%d" % e, align_bytes=64) for e in range(E)]
        w_planes = keep.tile([P, (E * PASSES // PLANES_PER_TILE) * H], U8, name="w_planes", align_bytes=64)
        grouped = [keep.tile([P, PASSES, T, PACK], BF16, name="grouped%d" % e, align_bytes=64) for e in range(E)]
        h_codes = [keep.tile([P, PASSES * T], U32, name="h_codes%d" % e, align_bytes=64) for e in range(E)]
        h_scales = [keep.tile([P, PASSES * T], U8, name="h_scales%d" % e, align_bytes=64) for e in range(E)]
        lowT_first = keep.tile([P, TOK_TILES, LOW_ROWS, LOW_BLOCKS // TOK_TILES], BF16, name="lowT_first")
        lowT_sb = keep.tile([P, TOK_TILES, P - LOW_ROWS, LOW_BLOCKS // TOK_TILES], BF16, name="lowT_sb")
        bT_sb = [keep.tile([P, H], BF16, name="bT_sb%d" % e) for e in range(E)]
        out_sb = [keep.tile([P, TOK_TILES, H], F32, name="out_sb%d" % e) for e in range(E)]
        ident_f32 = keep.tile([P, P], F32, name="ident_f32")
        ident_bf16 = keep.tile([P, P], BF16, name="ident_bf16")

        nc.vector.memset(w_planes[:].bitcast(I32), 0)
        make_identity(nc, ident_bf16[:])
        make_identity(nc, ident_f32[:])

        def load_lora_weight(e):
            nc.sync.dma_start(out=b_sb[e][:].rearrange("p c r -> p (c r)"), in_=b_view[e])

        def load_h(e):
            nc.sync.dma_start(out=h_sb[e][:], in_=h_view[e])

        def load_weight(e):
            nc.sync.dma_start(
                out=w_words[e][:].bitcast(I32),
                in_=W_d_words[PASSES * e : PASSES * (e + 1)].rearrange("g p n t -> p g (n t)").bitcast(I32),
            )

        def load_scale_planes(a):
            for quadrant in range(4):
                nc.sync.dma_start(
                    out=w_planes[32 * quadrant : 32 * quadrant + 16, a * H : (a + 1) * H].bitcast(I32),
                    in_=W_d_scales[
                        PLANES_PER_TILE * a : PLANES_PER_TILE * (a + 1), 4 * quadrant : 4 * quadrant + 4, :
                    ].bitcast(I32),
                )

        load_lora_weight(0)
        nc.sync.dma_start(out=low_sb[:].rearrange("p c r -> p (c r)"), in_=low_view)
        load_lora_weight(1)
        load_h(0)
        load_lora_weight(2)
        load_h(1)
        load_weight(0)
        load_scale_planes(0)
        load_lora_weight(3)
        load_h(2)
        load_weight(1)
        load_h(3)
        load_scale_planes(1)
        load_weight(2)
        load_weight(3)

        def transpose_lora_weight(e):
            bT_ps = psum.tile([P, B_BLOCKS, P], BF16, name="bT_ps", tag="bank")
            for c in range(B_BLOCKS):
                nc.tensor.transpose(bT_ps[:, c, :], b_sb[e][:, c, :], ident_bf16[:])
            copy = nc.vector.tensor_copy if e == 1 else nc.scalar.copy
            copy(
                out=bT_sb[e][:].rearrange("r (p c) -> r p c", c=B_BLOCKS),
                in_=bT_ps[:].rearrange("r c p -> r p c"),
            )

        def transpose_low():
            lowT_ps = psum.tile([P, LOW_BLOCKS, P], BF16, name="lowT_ps", tag="bank")
            for c in range(LOW_BLOCKS):
                nc.tensor.transpose(lowT_ps[:, c, :], low_sb[:, c, :], ident_bf16[:])
            sorted_view = lowT_ps[:].rearrange("r (b j) p -> r j p b", j=TOK_TILES)
            nc.vector.tensor_copy(out=lowT_first[:], in_=sorted_view[:, :, 0:LOW_ROWS, :])
            nc.vector.tensor_copy(out=lowT_sb[:], in_=sorted_view[:, :, LOW_ROWS:P, :])

        def transpose_h(e):
            for g in range(PASSES):
                hT_ps = psum.tile([P, 2, T], F32, name="hT_ps", tag="bank")
                for j in range(TOK_TILES):
                    h_pairs = h_sb[e][:, j, :].bitcast(F32)
                    for u in range(2):
                        nc.tensor.transpose(
                            hT_ps[:, u, j * P : (j + 1) * P],
                            h_pairs[:, WORDS * g + u : WORDS * (g + 1) : 2],
                            ident_f32[:],
                        )
                pairs_out = grouped[e][:, g].rearrange("p m t -> p (m t)").bitcast(F32)
                nc.scalar.copy(
                    out=pairs_out.rearrange("p (m u) -> p m u", u=2), in_=hT_ps[:].rearrange("p u m -> p m u")
                )

        def quantise_h(e):
            nc.vector.quantize_mx(
                out=h_codes[e][:].bitcast(FP8X4),
                scales=h_scales[e][:],
                in_=grouped[e][:].rearrange("p g m t -> p (g m t)"),
            )

        def lora_product(e, j, n):
            n_cols = slice(n * N_TILE, (n + 1) * N_TILE)
            delta = psum.tile([P, N_TILE], F32, name="delta", tag="bank")
            nc.tensor.matmul(
                delta[:],
                lhsT=(
                    lowT_first[:, j, :, :] if e == 0 else lowT_sb[:, j, LOW_ROWS * (e - 1) : LOW_ROWS * e, :]
                ).rearrange("r a b -> r (a b)"),
                rhs=bT_sb[e][:, n_cols],
                start=True,
                stop=True,
            )
            if n == 0 or e >= 2:
                nc.scalar.mul(out_sb[e][:, j, n_cols], delta[:], LORA_SCALE)
            else:
                nc.vector.tensor_scalar_mul(out_sb[e][:, j, n_cols], delta[:], LORA_SCALE)

        def mx_product(e, j, n):
            n_cols = slice(n * N_TILE, (n + 1) * N_TILE)
            acc = psum.tile([P, N_TILE], F32, name="acc", tag="bank")
            for g in range(PASSES):
                g_cat = PASSES * e + g
                first_row = 4 * (g_cat % PLANES_PER_TILE)
                first_col = (g_cat // PLANES_PER_TILE) * H + n * N_TILE
                tokens = slice(g * T + j * P, g * T + (j + 1) * P)
                nc.tensor.matmul_mx(
                    out=acc[:],
                    lhsT=h_codes[e][:, tokens].bitcast(FP8X4),
                    lhsT_scale=h_scales[e][:, tokens],
                    rhs=w_words[e][:, g, n_cols].bitcast(FP8X4),
                    rhs_scale=w_planes[first_row:P, first_col : first_col + N_TILE],
                    start=(g == 0),
                    stop=(g == PASSES - 1),
                )
            nc.vector.tensor_tensor(out=out_sb[e][:, j, n_cols], in0=acc[:], in1=out_sb[e][:, j, n_cols], op=ADD)

        def store(e, j, cols):
            nc.sync.dma_start(out=out_view[e][:, j, cols], in_=out_sb[e][:, j, cols])

        def store_expert(e):
            nc.sync.dma_start(
                out=out_view[e].rearrange("p j n -> p (j n)"), in_=out_sb[e][:].rearrange("p j n -> p (j n)")
            )

        def lora_products(e):
            for j in range(TOK_TILES):
                for n in range(N_TILES):
                    lora_product(e, j, n)

        def mx_products(e):
            for j in range(TOK_TILES):
                for n in range(N_TILES):
                    mx_product(e, j, n)
                if e >= WHOLE_STORES:
                    store(e, j, slice(0, H))
            if e < WHOLE_STORES:
                store_expert(e)

        transpose_lora_weight(0)
        transpose_low()
        transpose_lora_weight(1)
        lora_products(0)
        transpose_h(0)
        transpose_lora_weight(2)
        quantise_h(0)
        lora_products(1)
        transpose_h(1)
        quantise_h(1)
        mx_products(0)
        transpose_lora_weight(3)
        transpose_h(2)
        lora_products(2)
        quantise_h(2)
        mx_products(1)
        transpose_h(3)
        lora_products(3)
        quantise_h(3)
        mx_products(2)
        mx_products(3)
